import numpy as np
import ml_dtypes


def mxq(x, axis, fmt="e4m3"):
    dtype, down = {"e4m3": (ml_dtypes.float8_e4m3fn, 7), "e5m2": (ml_dtypes.float8_e5m2, 14)}[fmt]
    v = np.moveaxis(np.asarray(x, np.float32).astype(ml_dtypes.bfloat16).astype(np.float64), axis, -1)
    blocks = v.reshape(v.shape[:-1] + (-1, 32))
    amax = np.abs(blocks).max(-1, keepdims=True)
    byte = np.maximum(np.where(amax > 0, np.frexp(amax)[1] - 1 + 127, 0) - down, 1)
    scale = np.exp2(byte - 127.0)
    codes = (blocks / scale).astype(np.float32).astype(dtype).astype(np.float64)
    return np.moveaxis((codes * scale).reshape(v.shape), -1, axis)


WIDE = False


def mx_kscale(k):
    if not WIDE:
        return np.ones(k)
    levels = np.array([10, -10, 5, -5, 0])
    a = np.random.permutation(np.resize(levels, k // 512 * 4)).reshape(k // 512, 4)
    idx = np.arange(k)
    return np.exp2(a[idx // 512, idx % 128 // 32])


BF16 = ml_dtypes.bfloat16


def bf(x):
    return np.asarray(x, np.float32).astype(BF16)


def f64(x):
    return np.asarray(x).astype(np.float64)


B, E, H, A = 256, 1024, 1024, 2048


def sigmoid(v):
    return 1.0 / (1.0 + np.exp(-v))


def setup_inputs():
    rn = np.random.standard_normal
    se, sa = mx_kscale(E), mx_kscale(A)
    d = {"in_word": bf(rn((B, E)) * se), "last_hid_state": bf(rn((B, H))), "attended_state": bf(rn((B, A)) * sa)}
    for n in ("W", "Wz", "Wr"):
        d[n] = bf(rn((E, H)) * 0.6 / np.sqrt(E) / se[:, None])
    for n, g in (("U", 1.0), ("Uz", 0.6), ("Ur", 0.6)):
        d[n] = bf(rn((H, H)) * g / np.sqrt(H))
    for n in ("C", "Cz", "Cr"):
        d[n] = bf(rn((A, H)) * 0.6 / np.sqrt(A) / sa[:, None])
    for n in ("bw", "bwz", "bwr", "bu", "buz", "bur", "bc", "bcz", "bcr"):
        d[n] = bf(rn(H) * 0.4)
    return d


def reference(in_word, last_hid_state, attended_state, W, bw, Wz, bwz, Wr, bwr, U, bu, Uz, buz, Ur, bur, C, bc, Cz, bcz, Cr, bcr):
    h = f64(last_hid_state)
    xq = mxq(f64(in_word), 1, "e4m3")
    hq = mxq(h, 1, "e4m3")
    aq = mxq(f64(attended_state), 1, "e4m3")
    z = sigmoid(((xq @ mxq(f64(Wz), 0, "e4m3")) + f64(bwz))
                + ((hq @ mxq(f64(Uz), 0, "e4m3")) + f64(buz))
                + ((aq @ mxq(f64(Cz), 0, "e4m3")) + f64(bcz)))
    r = sigmoid(((xq @ mxq(f64(Wr), 0, "e4m3")) + f64(bwr))
                + ((hq @ mxq(f64(Ur), 0, "e4m3")) + f64(bur))
                + ((aq @ mxq(f64(Cr), 0, "e4m3")) + f64(bcr)))
    rh = r * h
    s_tilda = np.tanh(((xq @ mxq(f64(W), 0, "e4m3")) + f64(bw))
                      + ((mxq(rh, 1, "e4m3") @ mxq(f64(U), 0, "e4m3")) + f64(bu))
                      + ((aq @ mxq(f64(C), 0, "e4m3")) + f64(bc)))
    return (1.0 - z) * h + z * s_tilda

@@ -1,0 +1,286 @@
+from contextlib import ExitStack
+
+import concourse.mybir as mybir
+from concourse.masks import make_identity
+
+F32 = mybir.dt.float32
+BF16 = mybir.dt.bfloat16
+U32 = mybir.dt.uint32
+U8 = mybir.dt.uint8
+FP8X4 = mybir.dt.float8_e4m3fn_x4
+ACT = mybir.ActivationFunctionType
+ALU = mybir.AluOpType
+
+P = 128
+B = 256
+E = 1024
+H = 1024
+A = 2048
+KP = 512
+NBT = B // P
+NM = H // P
+
+FLOPS = 2 * B * (E + H + A) * H * 3
+
+RAW_BUFS = 8
+GRP_BUFS = 3
+Q_BUFS = 5
+
+
+def tile_attentiongrucell_pa_kernel(
+    tc, in_word, last_hid_state, attended_state,
+    W, Wz, Wr, U, Uz, Ur, C, Cz, Cr,
+    bw, bwz, bwr, bu, buz, bur, bc, bcz, bcr, out,
+):
+    nc = tc.nc
+    with ExitStack() as ctx:
+        const = ctx.enter_context(tc.tile_pool(name="const", bufs=1))
+        rawp = ctx.enter_context(tc.tile_pool(name="rawp", bufs=RAW_BUFS))
+        grpp = ctx.enter_context(tc.tile_pool(name="grpp", bufs=GRP_BUFS))
+        qp = ctx.enter_context(tc.tile_pool(name="qp", bufs=Q_BUFS))
+        ps = ctx.enter_context(tc.psum_pool(name="ps", bufs=1))
+        ctx.enter_context(tc.manual_schedule())
+
+        def bank(i, shape, dtype, name):
+            return ps.tile(shape, dtype, tag="bank%d" % i, name=name)
+
+        chunks = []
+        for gate, (wx, wh, wa) in enumerate(((Wr, Ur, Cr), (W, U, C), (Wz, Uz, Cz))):
+            part_x = [(wx, g, False, ("act", g)) for g in range(E // KP)]
+            part_a = [(wa, g, False, ("act", 4 + g)) for g in range(A // KP)]
+            if gate == 1:
+                part_h = [(wh, g, True, ("rh", g)) for g in range(H // KP)]
+                parts = part_x + part_a + part_h
+            else:
+                part_h = [(wh, g, False, ("act", 2 + g)) for g in range(H // KP)]
+                parts = part_x + part_h + part_a
+            for n, (w, g, by128, mov) in enumerate(parts):
+                chunks.append((w, g, by128, mov, gate, n == 0, n == len(parts) - 1))
+        NCH = len(chunks)
+
+        ident_f = const.tile([P, P], F32, name="ident_f")
+        make_identity(nc, ident_f[:])
+        ident_b = const.tile([P, P], BF16, name="ident_b")
+        btile = const.tile([P, P], BF16, name="btile")
+        nc.vector.memset(btile[:], 0.0)
+        warm_in = const.tile([P, 1], F32, name="warm_in")
+        warm_out = const.tile([P, 1], F32, name="warm_out")
+        nc.vector.memset(warm_in[:], 0.0)
+        nc.vector.tensor_copy(out=ident_b[:], in_=ident_f[:])
+        biases = (bwr, bw, bwz, bur, bu, buz, bcr, bc, bcz)
+
+        def load_bias(n):
+            nc.scalar.dma_start(
+                out=btile[n * NM:(n + 1) * NM, :],
+                in_=biases[n].rearrange("(i p) -> i p", p=P),
+            )
+
+        x_sb = const.tile([P, NBT, E], BF16, name="x_sb")
+        h_sb = const.tile([P, NBT, H], BF16, name="h_sb")
+        a_sb = const.tile([P, NBT, A], BF16, name="a_sb")
+        nc.sync.dma_start(out=x_sb[:], in_=in_word.rearrange("(t p) k -> p t k", p=P))
+        for n in range(4):
+            load_bias(n)
+        nc.scalar.activation(out=warm_out[:], in_=warm_in[:], func=ACT.Sigmoid)
+        nc.sync.dma_start(out=h_sb[:], in_=last_hid_state.rearrange("(t p) k -> p t k", p=P))
+        nc.sync.dma_start(out=a_sb[:], in_=attended_state.rearrange("(t p) k -> p t k", p=P))
+
+        raw = {}
+
+        def load(c):
+            w, g, by128 = chunks[c][0], chunks[c][1], chunks[c][2]
+            t = rawp.tile([P, 4, H], BF16, name="raw%d" % c, tag="raw")
+            rows = w[g * KP:(g + 1) * KP, :]
+            if by128:
+                src = rows.rearrange("(j p) n -> p j n", p=P)
+            else:
+                src = rows.rearrange("(p j) n -> p j n", j=4)
+            nc.sync.dma_start(out=t[:], in_=src)
+            raw[c] = t
+
+        load(0)
+        for n in range(4, 9):
+            load_bias(n)
+        for c in range(1, RAW_BUFS):
+            load(c)
+
+        actg = const.tile([P, 8 * 4 * B], BF16, name="actg", align_bytes=64)
+        actc = const.tile([P, 8 * B], U32, name="actc", align_bytes=64)
+        acts = const.tile([P, 8 * B], U8, name="acts", align_bytes=64)
+        hT = const.tile([P, NM, B], BF16, name="hT")
+
+        def word_transposes(src_sb, g, bk, name):
+            tw = bank(bk, [P, NBT, 2, P], F32, name)
+            words = src_sb[:].bitcast(F32).rearrange("p t (g q u) -> p t g u q", q=P, u=2)
+            for bt in range(NBT):
+                for u in range(2):
+                    nc.tensor.transpose(tw[:, bt, u, :], words[:, bt, g, u, :], ident_f[:])
+            return tw
+
+        def word_copy(copy, tw, pas):
+            dst = actg[:, pas * 4 * B:(pas + 1) * 4 * B].bitcast(F32)
+            copy(
+                out=dst.rearrange("p (t b u) -> p t b u", t=NBT, u=2),
+                in_=tw[:].rearrange("p t u b -> p t b u"),
+            )
+
+        def quant_act(p0, n):
+            nc.vector.quantize_mx(
+                out=actc[:, p0 * B:(p0 + n) * B].bitcast(FP8X4),
+                scales=acts[:, p0 * B:(p0 + n) * B],
+                in_=actg[:, p0 * 4 * B:(p0 + n) * 4 * B],
+            )
+
+        vcopy = nc.vector.tensor_copy
+        scopy = nc.scalar.copy
+
+        tx0 = word_transposes(x_sb, 0, 0, "tx0")
+        tx1 = word_transposes(x_sb, 1, 1, "tx1")
+        word_copy(vcopy, tx0, 0)
+        word_copy(scopy, tx1, 1)
+        th0 = word_transposes(h_sb, 0, 2, "th0")
+        th1 = word_transposes(h_sb, 1, 3, "th1")
+        quant_act(0, 2)
+        word_copy(scopy, th0, 2)
+        word_copy(vcopy, th1, 3)
+        for half in range(2):
+            hps = bank(4 + half, [P, 4, B], BF16, "hps%d" % half)
+            for i in range(4):
+                for bt in range(NBT):
+                    k0 = (half * 4 + i) * P
+                    nc.tensor.transpose(
+                        hps[:, i, bt * P:(bt + 1) * P], h_sb[:, bt, k0:k0 + P], ident_b[:]
+                    )
+            scopy(out=hT[:, half * 4:(half + 1) * 4, :], in_=hps[:])
+        bps = bank(6, [P, P], BF16, "bps")
+        nc.tensor.transpose(bps[:], btile[:], ident_b[:])
+        bT = const.tile([P, 9 * NM], F32, name="bT")
+        bsum = const.tile([P, 3 * NM], F32, name="bsum")
+        nc.vector.tensor_copy(out=bT[:], in_=bps[:, 0:9 * NM])
+        nc.vector.tensor_tensor(out=bsum[:], in0=bT[:, 0:24], in1=bT[:, 24:48], op=ALU.add)
+        nc.vector.tensor_tensor(out=bsum[:], in0=bsum[:], in1=bT[:, 48:72], op=ALU.add)
+        quant_act(2, 2)
+        ta0 = word_transposes(a_sb, 0, 7, "ta0")
+        ta1 = word_transposes(a_sb, 1, 0, "ta1")
+        ta2 = word_transposes(a_sb, 2, 1, "ta2")
+        ta3 = word_transposes(a_sb, 3, 2, "ta3")
+        word_copy(scopy, ta0, 4)
+        word_copy(vcopy, ta1, 5)
+        word_copy(scopy, ta2, 6)
+        word_copy(vcopy, ta3, 7)
+
+        grp = {}
+        cod = {}
+        scl = {}
+        acc = {}
+        r_sb = const.tile([P, NM, B], F32, name="r_sb")
+        c_sb = const.tile([P, NM, B], F32, name="c_sb")
+        z_sb = const.tile([P, NM, B], F32, name="z_sb")
+        o_sb = const.tile([P, NBT, H], F32, name="o_sb")
+        rhg = const.tile([P, 2 * 4 * B], BF16, name="rhg", align_bytes=64)
+        rhc = const.tile([P, 2 * B], U32, name="rhc", align_bytes=64)
+        rhs = const.tile([P, 2 * B], U8, name="rhs", align_bytes=64)
+
+        def regroup(c, split):
+            t = grpp.tile([P, 4 * H], BF16, name="grp%d" % c, tag="grp", align_bytes=64)
+            grp[c] = t
+            for copy, lo, hi in ((vcopy, 0, split), (scopy, split, H)):
+                if hi > lo:
+                    dst = t[:].rearrange("p (n j) -> p n j", j=4)[:, lo:hi, :]
+                    copy(
+                        out=dst.rearrange("p (c i) j -> p c j i", i=4),
+                        in_=raw[c][:, :, lo:hi].rearrange("p j (c i) -> p c j i", i=4),
+                    )
+
+        def quant(c):
+            cod[c] = qp.tile([P, H], U32, name="cod%d" % c, tag="cod", align_bytes=64)
+            scl[c] = qp.tile([P, H], U8, name="scl%d" % c, tag="scl", align_bytes=64)
+            nc.vector.quantize_mx(out=cod[c][:].bitcast(FP8X4), scales=scl[c][:], in_=grp[c][:])
+
+        def passes(c):
+            mov, gate, first, last = chunks[c][3], chunks[c][4], chunks[c][5], chunks[c][6]
+            kind, idx = mov
+            mc, ms = (actc, acts) if kind == "act" else (rhc, rhs)
+            for m in range(NM):
+                if first:
+                    acc[m] = bank(m, [P, B], F32, "acc%d_%d" % (gate, m))
+                nc.tensor.matmul_mx(
+                    out=acc[m][:],
+                    lhsT=cod[c][:, m * P:(m + 1) * P].bitcast(FP8X4),
+                    lhsT_scale=scl[c][:, m * P:(m + 1) * P],
+                    rhs=mc[:, idx * B:(idx + 1) * B].bitcast(FP8X4),
+                    rhs_scale=ms[:, idx * B:(idx + 1) * B],
+                    start=first,
+                    stop=last,
+                )
+
+        def gate_act(gate, dst, func):
+            for m in range(NM):
+                nc.scalar.activation(
+                    out=dst[:, m, :], in_=acc[m][:], func=func,
+                    bias=bsum[:, gate * NM + m:gate * NM + m + 1],
+                )
+
+        def rh_mul(g):
+            nc.vector.tensor_tensor(
+                out=rhg[:, g * 4 * B:(g + 1) * 4 * B].rearrange("p (b t) -> p b t", t=4),
+                in0=r_sb[:, 4 * g:4 * g + 4, :].rearrange("p t b -> p b t"),
+                in1=hT[:, 4 * g:4 * g + 4, :].rearrange("p t b -> p b t"),
+                op=ALU.mult,
+            )
+
+        def rh_quant():
+            nc.vector.quantize_mx(out=rhc[:].bitcast(FP8X4), scales=rhs[:], in_=rhg[:])
+
+        def c_minus_h(g):
+            nc.vector.tensor_tensor(
+                out=c_sb[:, 4 * g:4 * g + 4, :], in0=c_sb[:, 4 * g:4 * g + 4, :],
+                in1=hT[:, 4 * g:4 * g + 4, :], op=ALU.subtract,
+            )
+
+        SPLIT = 496
+        regroup(0, SPLIT)
+        load(RAW_BUFS)
+        quant_act(4, 4)
+        for s in range(NCH):
+            if s + 1 < NCH:
+                regroup(s + 1, SPLIT)
+                if s + 1 + RAW_BUFS < NCH:
+                    load(s + 1 + RAW_BUFS)
+            if s == 8:
+                gate_act(0, r_sb, ACT.Sigmoid)
+            if s == 16:
+                gate_act(1, c_sb, ACT.Tanh)
+            quant(s)
+            passes(s)
+            if s == 9:
+                rh_mul(0)
+                rh_mul(1)
+            if s == 10:
+                rh_quant()
+            if s == 17:
+                c_minus_h(0)
+                c_minus_h(1)
+
+        for half in range(2):
+            for i in range(4):
+                m = half * 4 + i
+                nc.scalar.activation(
+                    out=z_sb[:, m, :], in_=acc[m][:], func=ACT.Sigmoid,
+                    bias=bsum[:, 2 * NM + m:2 * NM + m + 1],
+                )
+                nc.vector.tensor_tensor(
+                    out=z_sb[:, m, :], in0=z_sb[:, m, :], in1=c_sb[:, m, :], op=ALU.mult
+                )
+            for bt in range(NBT):
+                pt = bank(half * 2 + bt, [P, 4 * P], F32, "po%d_%d" % (half, bt))
+                for i in range(4):
+                    m = half * 4 + i
+                    nc.tensor.transpose(
+                        pt[:, i * P:(i + 1) * P], z_sb[:, m, bt * P:(bt + 1) * P], ident_f[:]
+                    )
+                cols = slice(half * 4 * P, (half + 1) * 4 * P)
+                nc.vector.tensor_tensor(
+                    out=o_sb[:, bt, cols], in0=pt[:], in1=h_sb[:, bt, cols], op=ALU.add
+                )
+                nc.sync.dma_start(out=out[bt * P:(bt + 1) * P, cols], in_=o_sb[:, bt, cols])

@@ -24,7 +24,13 @@ FLOPS = 2 * B * (E + H + A) * H * 3
 
 RAW_BUFS = 8
 GRP_BUFS = 3
-Q_BUFS = 5
+Q_BUFS = 6
+SPLIT = 496
+TAIL_CHUNKS = 2
+NS = 4
+SW = H // NS
+MT = NM // NS
+TAIL_V = 200
 
 
 def tile_attentiongrucell_pa_kernel(
@@ -44,6 +50,9 @@ def tile_attentiongrucell_pa_kernel(
         def bank(i, shape, dtype, name):
             return ps.tile(shape, dtype, tag="bank%d" % i, name=name)
 
+        vcopy = nc.vector.tensor_copy
+        scopy = nc.scalar.copy
+
         chunks = []
         for gate, (wx, wh, wa) in enumerate(((Wr, Ur, Cr), (W, U, C), (Wz, Uz, Cz))):
             part_x = [(wx, g, False, ("act", g)) for g in range(E // KP)]
@@ -57,6 +66,7 @@ def tile_attentiongrucell_pa_kernel(
             for n, (w, g, by128, mov) in enumerate(parts):
                 chunks.append((w, g, by128, mov, gate, n == 0, n == len(parts) - 1))
         NCH = len(chunks)
+        NPLAIN = NCH - TAIL_CHUNKS
 
         ident_f = const.tile([P, P], F32, name="ident_f")
         make_identity(nc, ident_f[:])
@@ -78,16 +88,11 @@ def tile_attentiongrucell_pa_kernel(
         x_sb = const.tile([P, NBT, E], BF16, name="x_sb")
         h_sb = const.tile([P, NBT, H], BF16, name="h_sb")
         a_sb = const.tile([P, NBT, A], BF16, name="a_sb")
-        nc.sync.dma_start(out=x_sb[:], in_=in_word.rearrange("(t p) k -> p t k", p=P))
-        for n in range(4):
-            load_bias(n)
-        nc.scalar.activation(out=warm_out[:], in_=warm_in[:], func=ACT.Sigmoid)
-        nc.sync.dma_start(out=h_sb[:], in_=last_hid_state.rearrange("(t p) k -> p t k", p=P))
-        nc.sync.dma_start(out=a_sb[:], in_=attended_state.rearrange("(t p) k -> p t k", p=P))
-
         raw = {}
 
         def load(c):
+            if c >= NCH:
+                return
             w, g, by128 = chunks[c][0], chunks[c][1], chunks[c][2]
             t = rawp.tile([P, 4, H], BF16, name="raw%d" % c, tag="raw")
             rows = w[g * KP:(g + 1) * KP, :]
@@ -98,16 +103,36 @@ def tile_attentiongrucell_pa_kernel(
             nc.sync.dma_start(out=t[:], in_=src)
             raw[c] = t
 
+        nc.sync.dma_start(out=x_sb[:], in_=in_word.rearrange("(t p) k -> p t k", p=P))
+        for n in range(4):
+            load_bias(n)
+        nc.scalar.activation(out=warm_out[:], in_=warm_in[:], func=ACT.Sigmoid)
         load(0)
+        nc.sync.dma_start(out=h_sb[:], in_=last_hid_state.rearrange("(t p) k -> p t k", p=P))
+        load(1)
         for n in range(4, 9):
             load_bias(n)
-        for c in range(1, RAW_BUFS):
+        nc.sync.dma_start(out=a_sb[:], in_=attended_state.rearrange("(t p) k -> p t k", p=P))
+        for c in range(2, RAW_BUFS):
             load(c)
 
         actg = const.tile([P, 8 * 4 * B], BF16, name="actg", align_bytes=64)
         actc = const.tile([P, 8 * B], U32, name="actc", align_bytes=64)
         acts = const.tile([P, 8 * B], U8, name="acts", align_bytes=64)
         hT = const.tile([P, NM, B], BF16, name="hT")
+        bT = const.tile([P, 9 * NM], F32, name="bT")
+        bsum = const.tile([P, 3 * NM], F32, name="bsum")
+        r_sb = const.tile([P, NM, B], F32, name="r_sb")
+        c_sb = const.tile([P, NM, B], F32, name="c_sb")
+        z_sb = const.tile([P, NM, B], F32, name="z_sb")
+        o_sb = const.tile([P, NBT, H], F32, name="o_sb")
+        rhg = const.tile([P, 2 * 4 * B], BF16, name="rhg", align_bytes=64)
+        rhc = const.tile([P, 2 * B], U32, name="rhc", align_bytes=64)
+        rhs = const.tile([P, 2 * B], U8, name="rhs", align_bytes=64)
+        grp = {}
+        cod = {}
+        scl = {}
+        acc = {}
 
         def word_transposes(src_sb, g, bk, name):
             tw = bank(bk, [P, NBT, 2, P], F32, name)
@@ -131,95 +156,62 @@ def tile_attentiongrucell_pa_kernel(
                 in_=actg[:, p0 * 4 * B:(p0 + n) * 4 * B],
             )
 
-        vcopy = nc.vector.tensor_copy
-        scopy = nc.scalar.copy
-
-        tx0 = word_transposes(x_sb, 0, 0, "tx0")
-        tx1 = word_transposes(x_sb, 1, 1, "tx1")
-        word_copy(vcopy, tx0, 0)
-        word_copy(scopy, tx1, 1)
-        th0 = word_transposes(h_sb, 0, 2, "th0")
-        th1 = word_transposes(h_sb, 1, 3, "th1")
-        quant_act(0, 2)
-        word_copy(scopy, th0, 2)
-        word_copy(vcopy, th1, 3)
-        for half in range(2):
-            hps = bank(4 + half, [P, 4, B], BF16, "hps%d" % half)
+        def h_transposes(half, bk):
+            hps = bank(bk, [P, 4, B], BF16, "hps%d" % half)
             for i in range(4):
                 for bt in range(NBT):
                     k0 = (half * 4 + i) * P
                     nc.tensor.transpose(
                         hps[:, i, bt * P:(bt + 1) * P], h_sb[:, bt, k0:k0 + P], ident_b[:]
                     )
-            scopy(out=hT[:, half * 4:(half + 1) * 4, :], in_=hps[:])
-        bps = bank(6, [P, P], BF16, "bps")
-        nc.tensor.transpose(bps[:], btile[:], ident_b[:])
-        bT = const.tile([P, 9 * NM], F32, name="bT")
-        bsum = const.tile([P, 3 * NM], F32, name="bsum")
-        nc.vector.tensor_copy(out=bT[:], in_=bps[:, 0:9 * NM])
-        nc.vector.tensor_tensor(out=bsum[:], in0=bT[:, 0:24], in1=bT[:, 24:48], op=ALU.add)
-        nc.vector.tensor_tensor(out=bsum[:], in0=bsum[:], in1=bT[:, 48:72], op=ALU.add)
-        quant_act(2, 2)
-        ta0 = word_transposes(a_sb, 0, 7, "ta0")
-        ta1 = word_transposes(a_sb, 1, 0, "ta1")
-        ta2 = word_transposes(a_sb, 2, 1, "ta2")
-        ta3 = word_transposes(a_sb, 3, 2, "ta3")
-        word_copy(scopy, ta0, 4)
-        word_copy(vcopy, ta1, 5)
-        word_copy(scopy, ta2, 6)
-        word_copy(vcopy, ta3, 7)
+            return hps
 
-        grp = {}
-        cod = {}
-        scl = {}
-        acc = {}
-        r_sb = const.tile([P, NM, B], F32, name="r_sb")
-        c_sb = const.tile([P, NM, B], F32, name="c_sb")
-        z_sb = const.tile([P, NM, B], F32, name="z_sb")
-        o_sb = const.tile([P, NBT, H], F32, name="o_sb")
-        rhg = const.tile([P, 2 * 4 * B], BF16, name="rhg", align_bytes=64)
-        rhc = const.tile([P, 2 * B], U32, name="rhc", align_bytes=64)
-        rhs = const.tile([P, 2 * B], U8, name="rhs", align_bytes=64)
+        def regroup_cols(copy, dst, src):
+            copy(
+                out=dst.rearrange("p (c i j) -> p c j i", i=4, j=4),
+                in_=src.rearrange("p j (c i) -> p c j i", i=4),
+            )
 
-        def regroup(c, split):
+        def regroup(c):
             t = grpp.tile([P, 4 * H], BF16, name="grp%d" % c, tag="grp", align_bytes=64)
             grp[c] = t
-            for copy, lo, hi in ((vcopy, 0, split), (scopy, split, H)):
-                if hi > lo:
-                    dst = t[:].rearrange("p (n j) -> p n j", j=4)[:, lo:hi, :]
-                    copy(
-                        out=dst.rearrange("p (c i) j -> p c j i", i=4),
-                        in_=raw[c][:, :, lo:hi].rearrange("p j (c i) -> p c j i", i=4),
-                    )
+            regroup_cols(vcopy, t[:, 0:4 * SPLIT], raw[c][:, :, 0:SPLIT])
+            regroup_cols(scopy, t[:, 4 * SPLIT:4 * H], raw[c][:, :, SPLIT:H])
+            load(c + RAW_BUFS)
 
-        def quant(c):
+        def new_codes(c):
             cod[c] = qp.tile([P, H], U32, name="cod%d" % c, tag="cod", align_bytes=64)
             scl[c] = qp.tile([P, H], U8, name="scl%d" % c, tag="scl", align_bytes=64)
+
+        def quant(c):
+            new_codes(c)
             nc.vector.quantize_mx(out=cod[c][:].bitcast(FP8X4), scales=scl[c][:], in_=grp[c][:])
 
-        def passes(c):
+        def one_pass(c, m, codes, scales, col):
             mov, gate, first, last = chunks[c][3], chunks[c][4], chunks[c][5], chunks[c][6]
             kind, idx = mov
             mc, ms = (actc, acts) if kind == "act" else (rhc, rhs)
-            for m in range(NM):
-                if first:
-                    acc[m] = bank(m, [P, B], F32, "acc%d_%d" % (gate, m))
-                nc.tensor.matmul_mx(
-                    out=acc[m][:],
-                    lhsT=cod[c][:, m * P:(m + 1) * P].bitcast(FP8X4),
-                    lhsT_scale=scl[c][:, m * P:(m + 1) * P],
-                    rhs=mc[:, idx * B:(idx + 1) * B].bitcast(FP8X4),
-                    rhs_scale=ms[:, idx * B:(idx + 1) * B],
-                    start=first,
-                    stop=last,
-                )
+            if first:
+                acc[m] = bank(m, [P, B], F32, "acc%d_%d" % (gate, m))
+            nc.tensor.matmul_mx(
+                out=acc[m][:],
+                lhsT=codes[:, col:col + P].bitcast(FP8X4),
+                lhsT_scale=scales[:, col:col + P],
+                rhs=mc[:, idx * B:(idx + 1) * B].bitcast(FP8X4),
+                rhs_scale=ms[:, idx * B:(idx + 1) * B],
+                start=first,
+                stop=last,
+            )
 
-        def gate_act(gate, dst, func):
+        def passes(c):
             for m in range(NM):
-                nc.scalar.activation(
-                    out=dst[:, m, :], in_=acc[m][:], func=func,
-                    bias=bsum[:, gate * NM + m:gate * NM + m + 1],
-                )
+                one_pass(c, m, cod[c], scl[c], m * P)
+
+        def gate_act(gate, m, dst, func):
+            nc.scalar.activation(
+                out=dst[:, m, :], in_=acc[m][:], func=func,
+                bias=bsum[:, gate * NM + m:gate * NM + m + 1],
+            )
 
         def rh_mul(g):
             nc.vector.tensor_tensor(
@@ -229,58 +221,120 @@ def tile_attentiongrucell_pa_kernel(
                 op=ALU.mult,
             )
 
-        def rh_quant():
-            nc.vector.quantize_mx(out=rhc[:].bitcast(FP8X4), scales=rhs[:], in_=rhg[:])
-
         def c_minus_h(g):
             nc.vector.tensor_tensor(
                 out=c_sb[:, 4 * g:4 * g + 4, :], in0=c_sb[:, 4 * g:4 * g + 4, :],
                 in1=hT[:, 4 * g:4 * g + 4, :], op=ALU.subtract,
             )
 
-        SPLIT = 496
-        regroup(0, SPLIT)
-        load(RAW_BUFS)
+        tx0 = word_transposes(x_sb, 0, 0, "tx0")
+        tx1 = word_transposes(x_sb, 1, 1, "tx1")
+        word_copy(vcopy, tx0, 0)
+        word_copy(scopy, tx1, 1)
+        th0 = word_transposes(h_sb, 0, 2, "th0")
+        th1 = word_transposes(h_sb, 1, 3, "th1")
+        hps0 = h_transposes(0, 4)
+        hps1 = h_transposes(1, 5)
+        bps = bank(6, [P, P], BF16, "bps")
+        nc.tensor.transpose(bps[:], btile[:], ident_b[:])
+        ta0 = word_transposes(a_sb, 0, 7, "ta0")
+        ta1 = word_transposes(a_sb, 1, 0, "ta1")
+        ta2 = word_transposes(a_sb, 2, 1, "ta2")
+        quant_act(0, 2)
+        regroup(0)
+        word_copy(scopy, th0, 2)
+        word_copy(vcopy, th1, 3)
+        ta3 = word_transposes(a_sb, 3, 2, "ta3")
+        regroup(1)
+        quant(0)
+        scopy(out=hT[:, 0:4, :], in_=hps0[:])
+        scopy(out=hT[:, 4:8, :], in_=hps1[:])
+        quant_act(2, 2)
+        nc.vector.tensor_copy(out=bT[:], in_=bps[:, 0:9 * NM])
+        nc.vector.tensor_tensor(out=bsum[:], in0=bT[:, 0:24], in1=bT[:, 24:48], op=ALU.add)
+        nc.vector.tensor_tensor(out=bsum[:], in0=bsum[:], in1=bT[:, 48:72], op=ALU.add)
+        regroup(2)
+        quant(1)
+        word_copy(scopy, ta0, 4)
+        word_copy(vcopy, ta1, 5)
+        word_copy(scopy, ta2, 6)
+        word_copy(vcopy, ta3, 7)
+        regroup(3)
+        quant(2)
         quant_act(4, 4)
-        for s in range(NCH):
-            if s + 1 < NCH:
-                regroup(s + 1, SPLIT)
-                if s + 1 + RAW_BUFS < NCH:
-                    load(s + 1 + RAW_BUFS)
+        passes(0)
+        passes(1)
+        passes(2)
+
+        for s in range(3, NPLAIN):
+            if s + 1 < NPLAIN:
+                regroup(s + 1)
             if s == 8:
-                gate_act(0, r_sb, ACT.Sigmoid)
+                for m in range(NM):
+                    gate_act(0, m, r_sb, ACT.Sigmoid)
             if s == 16:
-                gate_act(1, c_sb, ACT.Tanh)
+                for m in range(NM):
+                    gate_act(1, m, c_sb, ACT.Tanh)
             quant(s)
             passes(s)
             if s == 9:
                 rh_mul(0)
                 rh_mul(1)
             if s == 10:
-                rh_quant()
+                nc.vector.quantize_mx(out=rhc[:].bitcast(FP8X4), scales=rhs[:], in_=rhg[:])
             if s == 17:
                 c_minus_h(0)
                 c_minus_h(1)
 
-        for half in range(2):
-            for i in range(4):
-                m = half * 4 + i
-                nc.scalar.activation(
-                    out=z_sb[:, m, :], in_=acc[m][:], func=ACT.Sigmoid,
-                    bias=bsum[:, 2 * NM + m:2 * NM + m + 1],
-                )
-                nc.vector.tensor_tensor(
-                    out=z_sb[:, m, :], in0=z_sb[:, m, :], in1=c_sb[:, m, :], op=ALU.mult
-                )
+        out_v = out.rearrange("(t p) n -> p t n", p=P)
+        po = {}
+
+        def tail_a(sl):
+            if sl % 2 == 0:
+                new_codes(NPLAIN + sl // 2)
+            codes, scales = cod[NPLAIN + sl // 2], scl[NPLAIN + sl // 2]
+            g0 = sl * TAIL_CHUNKS * 4 * SW
+            for k in reversed(range(TAIL_CHUNKS)):
+                src = raw[NPLAIN + k]
+                dst = actg[:, g0 + k * 4 * SW:g0 + (k + 1) * 4 * SW]
+                nv = TAIL_V if k == TAIL_CHUNKS - 1 else 0
+                cut = SW - nv
+                regroup_cols(scopy, dst[:, 0:4 * cut], src[:, :, sl * SW:sl * SW + cut])
+                if nv > 0:
+                    regroup_cols(vcopy, dst[:, 4 * cut:4 * SW], src[:, :, sl * SW + cut:(sl + 1) * SW])
+            q0 = (sl % 2) * TAIL_CHUNKS * SW
+            nc.vector.quantize_mx(
+                out=codes[:, q0:q0 + TAIL_CHUNKS * SW].bitcast(FP8X4),
+                scales=scales[:, q0:q0 + TAIL_CHUNKS * SW],
+                in_=actg[:, g0:g0 + TAIL_CHUNKS * 4 * SW],
+            )
+            for i in range(MT):
+                for k in range(TAIL_CHUNKS):
+                    one_pass(NPLAIN + k, sl * MT + i, codes, scales, q0 + k * SW + i * P)
+
+        def tail_b(sl):
+            ms = slice(sl * MT, (sl + 1) * MT)
+            for i in range(MT):
+                gate_act(2, sl * MT + i, z_sb, ACT.Sigmoid)
+            nc.vector.tensor_tensor(out=z_sb[:, ms, :], in0=z_sb[:, ms, :], in1=c_sb[:, ms, :], op=ALU.mult)
+            po[sl] = bank(sl * MT, [P, NBT, SW], F32, "po%d" % sl)
             for bt in range(NBT):
-                pt = bank(half * 2 + bt, [P, 4 * P], F32, "po%d_%d" % (half, bt))
-                for i in range(4):
-                    m = half * 4 + i
+                for i in range(MT):
                     nc.tensor.transpose(
-                        pt[:, i * P:(i + 1) * P], z_sb[:, m, bt * P:(bt + 1) * P], ident_f[:]
+                        po[sl][:, bt, i * P:(i + 1) * P],
+                        z_sb[:, sl * MT + i, bt * P:(bt + 1) * P],
+                        ident_f[:],
                     )
-                cols = slice(half * 4 * P, (half + 1) * 4 * P)
-                nc.vector.tensor_tensor(
-                    out=o_sb[:, bt, cols], in0=pt[:], in1=h_sb[:, bt, cols], op=ALU.add
-                )
-                nc.sync.dma_start(out=out[bt * P:(bt + 1) * P, cols], in_=o_sb[:, bt, cols])
+
+        def tail_c(sl):
+            cols = slice(sl * SW, (sl + 1) * SW)
+            nc.vector.tensor_tensor(out=o_sb[:, :, cols], in0=po[sl][:], in1=h_sb[:, :, cols], op=ALU.add)
+            nc.sync.dma_start(out=out_v[:, :, cols], in_=o_sb[:, :, cols])
+
+        for i in range(NS + 3):
+            if i < NS:
+                tail_a(i)
+            if 0 <= i - 2 < NS:
+                tail_b(i - 2)
+            if 0 <= i - 3 < NS:
+                tail_c(i - 3)

@@ -24,13 +24,16 @@ FLOPS = 2 * B * (E + H + A) * H * 3
 
 RAW_BUFS = 8
 GRP_BUFS = 3
-Q_BUFS = 6
+Q_BUFS = 10
 SPLIT = 496
+SPLIT_D = 416
+DET_COLS = 256
+NLIVE = 6
 TAIL_CHUNKS = 2
 NS = 4
 SW = H // NS
 MT = NM // NS
-TAIL_V = 200
+TAIL_V = 256
 
 
 def tile_attentiongrucell_pa_kernel(
@@ -68,6 +71,10 @@ def tile_attentiongrucell_pa_kernel(
         NCH = len(chunks)
         NPLAIN = NCH - TAIL_CHUNKS
 
+        def is_det(c):
+            gate, n = divmod(c, 8)
+            return 0 <= c < NCH and 2 <= n <= (7 if gate < 2 else 5)
+
         ident_f = const.tile([P, P], F32, name="ident_f")
         make_identity(nc, ident_f[:])
         ident_b = const.tile([P, P], BF16, name="ident_b")
@@ -87,7 +94,7 @@ def tile_attentiongrucell_pa_kernel(
 
         x_sb = const.tile([P, NBT, E], BF16, name="x_sb")
         h_sb = const.tile([P, NBT, H], BF16, name="h_sb")
-        a_sb = const.tile([P, NBT, A], BF16, name="a_sb")
+        a_sb = const.tile([P, NBT, A], BF16, name="a_sb", tag="a_o")
         raw = {}
 
         def load(c):
@@ -122,10 +129,8 @@ def tile_attentiongrucell_pa_kernel(
         hT = const.tile([P, NM, B], BF16, name="hT")
         bT = const.tile([P, 9 * NM], F32, name="bT")
         bsum = const.tile([P, 3 * NM], F32, name="bsum")
-        r_sb = const.tile([P, NM, B], F32, name="r_sb")
+        r_sb = const.tile([P, NM, B], F32, name="r_sb", tag="r_z")
         c_sb = const.tile([P, NM, B], F32, name="c_sb")
-        z_sb = const.tile([P, NM, B], F32, name="z_sb")
-        o_sb = const.tile([P, NBT, H], F32, name="o_sb")
         rhg = const.tile([P, 2 * 4 * B], BF16, name="rhg", align_bytes=64)
         rhc = const.tile([P, 2 * B], U32, name="rhc", align_bytes=64)
         rhs = const.tile([P, 2 * B], U8, name="rhs", align_bytes=64)
@@ -133,6 +138,7 @@ def tile_attentiongrucell_pa_kernel(
         cod = {}
         scl = {}
         acc = {}
+        det = {}
 
         def word_transposes(src_sb, g, bk, name):
             tw = bank(bk, [P, NBT, 2, P], F32, name)
@@ -175,9 +181,26 @@ def tile_attentiongrucell_pa_kernel(
         def regroup(c):
             t = grpp.tile([P, 4 * H], BF16, name="grp%d" % c, tag="grp", align_bytes=64)
             grp[c] = t
-            regroup_cols(vcopy, t[:, 0:4 * SPLIT], raw[c][:, :, 0:SPLIT])
-            regroup_cols(scopy, t[:, 4 * SPLIT:4 * H], raw[c][:, :, SPLIT:H])
+            cut = SPLIT_D if is_det(c) else SPLIT
+            top = H - DET_COLS if is_det(c) else H
+            regroup_cols(vcopy, t[:, 0:4 * cut], raw[c][:, :, 0:cut])
+            regroup_cols(scopy, t[:, 4 * cut:4 * top], raw[c][:, :, cut:top])
+            if is_det(c):
+                scopy(out=t[:, 4 * top:4 * H], in_=det[c][:].rearrange("p n j -> p (n j)"))
             load(c + RAW_BUFS)
+
+        def detour(c):
+            if not is_det(c):
+                return
+            det[c] = bank(NLIVE + c % 2, [P, DET_COLS, 4], BF16, "det%d" % c)
+            for a in range(2):
+                nc.tensor.matmul(
+                    out=det[c][:, :, 2 * a:2 * a + 2].rearrange("p n j -> p j n"),
+                    lhsT=ident_b[:],
+                    rhs=raw[c][:, 2 * a:2 * a + 2, H - DET_COLS:H],
+                    start=True,
+                    stop=True,
+                )
 
         def new_codes(c):
             cod[c] = qp.tile([P, H], U32, name="cod%d" % c, tag="cod", align_bytes=64)
@@ -204,8 +227,12 @@ def tile_attentiongrucell_pa_kernel(
             )
 
         def passes(c):
-            for m in range(NM):
+            for m in range(NLIVE):
                 one_pass(c, m, cod[c], scl[c], m * P)
+            if not is_det(c + 1) and is_det(c):
+                for m in range(NLIVE, NM):
+                    for cc in range(c - c % 8, c + 1):
+                        one_pass(cc, m, cod[cc], scl[cc], m * P)
 
         def gate_act(gate, m, dst, func):
             nc.scalar.activation(
@@ -235,33 +262,36 @@ def tile_attentiongrucell_pa_kernel(
         th1 = word_transposes(h_sb, 1, 3, "th1")
         hps0 = h_transposes(0, 4)
         hps1 = h_transposes(1, 5)
-        bps = bank(6, [P, P], BF16, "bps")
-        nc.tensor.transpose(bps[:], btile[:], ident_b[:])
-        ta0 = word_transposes(a_sb, 0, 7, "ta0")
-        ta1 = word_transposes(a_sb, 1, 0, "ta1")
-        ta2 = word_transposes(a_sb, 2, 1, "ta2")
+        ta0 = word_transposes(a_sb, 0, 0, "ta0")
+        ta1 = word_transposes(a_sb, 1, 1, "ta1")
         quant_act(0, 2)
         regroup(0)
         word_copy(scopy, th0, 2)
         word_copy(vcopy, th1, 3)
-        ta3 = word_transposes(a_sb, 3, 2, "ta3")
+        ta2 = word_transposes(a_sb, 2, 2, "ta2")
+        ta3 = word_transposes(a_sb, 3, 3, "ta3")
         regroup(1)
         quant(0)
         scopy(out=hT[:, 0:4, :], in_=hps0[:])
         scopy(out=hT[:, 4:8, :], in_=hps1[:])
+        bps = bank(4, [P, P], BF16, "bps")
+        nc.tensor.transpose(bps[:], btile[:], ident_b[:])
+        detour(2)
         quant_act(2, 2)
-        nc.vector.tensor_copy(out=bT[:], in_=bps[:, 0:9 * NM])
-        nc.vector.tensor_tensor(out=bsum[:], in0=bT[:, 0:24], in1=bT[:, 24:48], op=ALU.add)
-        nc.vector.tensor_tensor(out=bsum[:], in0=bsum[:], in1=bT[:, 48:72], op=ALU.add)
         regroup(2)
         quant(1)
+        detour(3)
         word_copy(scopy, ta0, 4)
         word_copy(vcopy, ta1, 5)
         word_copy(scopy, ta2, 6)
         word_copy(vcopy, ta3, 7)
         regroup(3)
         quant(2)
+        nc.vector.tensor_copy(out=bT[:], in_=bps[:, 0:9 * NM])
+        nc.vector.tensor_tensor(out=bsum[:], in0=bT[:, 0:24], in1=bT[:, 24:48], op=ALU.add)
+        nc.vector.tensor_tensor(out=bsum[:], in0=bsum[:], in1=bT[:, 48:72], op=ALU.add)
         quant_act(4, 4)
+        detour(4)
         passes(0)
         passes(1)
         passes(2)
@@ -275,6 +305,7 @@ def tile_attentiongrucell_pa_kernel(
             if s == 16:
                 for m in range(NM):
                     gate_act(1, m, c_sb, ACT.Tanh)
+            detour(s + 2)
             quant(s)
             passes(s)
             if s == 9:
@@ -288,6 +319,8 @@ def tile_attentiongrucell_pa_kernel(
 
         out_v = out.rearrange("(t p) n -> p t n", p=P)
         po = {}
+        z_sb = const.tile([P, NM, B], F32, name="z_sb", tag="r_z")
+        o_sb = const.tile([P, NBT, H], F32, name="o_sb", tag="a_o")
 
         def tail_a(sl):
             if sl % 2 == 0:
@@ -299,7 +332,8 @@ def tile_attentiongrucell_pa_kernel(
                 dst = actg[:, g0 + k * 4 * SW:g0 + (k + 1) * 4 * SW]
                 nv = TAIL_V if k == TAIL_CHUNKS - 1 else 0
                 cut = SW - nv
-                regroup_cols(scopy, dst[:, 0:4 * cut], src[:, :, sl * SW:sl * SW + cut])
+                if cut > 0:
+                    regroup_cols(scopy, dst[:, 0:4 * cut], src[:, :, sl * SW:sl * SW + cut])
                 if nv > 0:
                     regroup_cols(vcopy, dst[:, 4 * cut:4 * SW], src[:, :, sl * SW + cut:(sl + 1) * SW])
             q0 = (sl % 2) * TAIL_CHUNKS * SW

@@ -229,10 +229,13 @@ def tile_attentiongrucell_pa_kernel(
         def passes(c):
             for m in range(NLIVE):
                 one_pass(c, m, cod[c], scl[c], m * P)
-            if not is_det(c + 1) and is_det(c):
-                for m in range(NLIVE, NM):
-                    for cc in range(c - c % 8, c + 1):
-                        one_pass(cc, m, cod[cc], scl[cc], m * P)
+            if chunks[c][6]:
+                catch_up(c)
+
+        def catch_up(c):
+            for m in range(NLIVE, NM):
+                for cc in range(c - c % 8, c + 1):
+                    one_pass(cc, m, cod[cc], scl[cc], m * P)
 
         def gate_act(gate, m, dst, func):
             nc.scalar.activation(
@@ -342,6 +345,8 @@ def tile_attentiongrucell_pa_kernel(
                 scales=scales[:, q0:q0 + TAIL_CHUNKS * SW],
                 in_=actg[:, g0:g0 + TAIL_CHUNKS * 4 * SW],
             )
+            if sl == 1:
+                catch_up(NPLAIN - 1)
             for i in range(MT):
                 for k in range(TAIL_CHUNKS):
                     one_pass(NPLAIN + k, sl * MT + i, codes, scales, q0 + k * SW + i * P)
@@ -353,22 +358,29 @@ def tile_attentiongrucell_pa_kernel(
             nc.vector.tensor_tensor(out=z_sb[:, ms, :], in0=z_sb[:, ms, :], in1=c_sb[:, ms, :], op=ALU.mult)
             po[sl] = bank(sl * MT, [P, NBT, SW], F32, "po%d" % sl)
             for bt in range(NBT):
+                nc.tensor.matmul(
+                    out=po[sl][:, bt, :], lhsT=ident_b[:], rhs=h_sb[:, bt, sl * SW:(sl + 1) * SW],
+                    start=True, stop=False,
+                )
                 for i in range(MT):
-                    nc.tensor.transpose(
-                        po[sl][:, bt, i * P:(i + 1) * P],
-                        z_sb[:, sl * MT + i, bt * P:(bt + 1) * P],
-                        ident_f[:],
+                    nc.tensor.matmul(
+                        out=po[sl][:, bt, i * P:(i + 1) * P],
+                        lhsT=z_sb[:, sl * MT + i, bt * P:(bt + 1) * P],
+                        rhs=ident_f[:],
+                        is_transpose=True,
+                        start=False,
+                        stop=(i == MT - 1),
                     )
 
         def tail_c(sl):
             cols = slice(sl * SW, (sl + 1) * SW)
-            nc.vector.tensor_tensor(out=o_sb[:, :, cols], in0=po[sl][:], in1=h_sb[:, :, cols], op=ALU.add)
+            scopy(out=o_sb[:, :, cols], in_=po[sl][:])
             nc.sync.dma_start(out=out_v[:, :, cols], in_=o_sb[:, :, cols])
 
-        for i in range(NS + 3):
+        for i in range(NS + 4):
             if i < NS:
                 tail_a(i)
             if 0 <= i - 2 < NS:
                 tail_b(i - 2)
-            if 0 <= i - 3 < NS:
-                tail_c(i - 3)
+            if 0 <= i - 4 < NS:
+                tail_c(i - 4)

@@ -48,7 +48,6 @@ def tile_attentiongrucell_pa_kernel(
         grpp = ctx.enter_context(tc.tile_pool(name="grpp", bufs=GRP_BUFS))
         qp = ctx.enter_context(tc.tile_pool(name="qp", bufs=Q_BUFS))
         ps = ctx.enter_context(tc.psum_pool(name="ps", bufs=1))
-        ctx.enter_context(tc.manual_schedule())
 
         def bank(i, shape, dtype, name):
             return ps.tile(shape, dtype, tag="bank%d" % i, name=name)

@@ -173,8 +173,8 @@ def tile_attentiongrucell_pa_kernel(
 
         def regroup_cols(copy, dst, src):
             copy(
-                out=dst.rearrange("p (c i j) -> p c j i", i=4, j=4),
-                in_=src.rearrange("p j (c i) -> p c j i", i=4),
+                out=dst.rearrange("p (c i j) -> p c j i", i=8, j=4),
+                in_=src.rearrange("p j (c i) -> p c j i", i=8),
             )
 
         def regroup(c):

@@ -23,7 +23,7 @@ NM = H // P
 FLOPS = 2 * B * (E + H + A) * H * 3
 
 RAW_BUFS = 8
-GRP_BUFS = 3
+GRP_BUFS = 4
 Q_BUFS = 10
 SPLIT = 496
 SPLIT_D = 416
@@ -244,9 +244,9 @@ def tile_attentiongrucell_pa_kernel(
 
         def rh_mul(g):
             nc.vector.tensor_tensor(
-                out=rhg[:, g * 4 * B:(g + 1) * 4 * B].rearrange("p (b t) -> p b t", t=4),
-                in0=r_sb[:, 4 * g:4 * g + 4, :].rearrange("p t b -> p b t"),
-                in1=hT[:, 4 * g:4 * g + 4, :].rearrange("p t b -> p b t"),
+                out=rhg[:, g * 4 * B:(g + 1) * 4 * B].rearrange("p (c i t) -> p c t i", i=4, t=4),
+                in0=r_sb[:, 4 * g:4 * g + 4, :].rearrange("p t (c i) -> p c t i", i=4),
+                in1=hT[:, 4 * g:4 * g + 4, :].rearrange("p t (c i) -> p c t i", i=4),
                 op=ALU.mult,
             )
 
@@ -310,14 +310,12 @@ def tile_attentiongrucell_pa_kernel(
             detour(s + 2)
             quant(s)
             passes(s)
-            if s == 9:
-                rh_mul(0)
-                rh_mul(1)
-            if s == 10:
+            if s in (9, 10):
+                rh_mul(s - 9)
+            if s == 11:
                 nc.vector.quantize_mx(out=rhc[:].bitcast(FP8X4), scales=rhs[:], in_=rhg[:])
-            if s == 17:
-                c_minus_h(0)
-                c_minus_h(1)
+            if s in (17, 18):
+                c_minus_h(s - 17)
 
         out_v = out.rearrange("(t p) n -> p t n", p=P)
         po = {}
@@ -356,11 +354,10 @@ def tile_attentiongrucell_pa_kernel(
                 gate_act(2, sl * MT + i, z_sb, ACT.Sigmoid)
             nc.vector.tensor_tensor(out=z_sb[:, ms, :], in0=z_sb[:, ms, :], in1=c_sb[:, ms, :], op=ALU.mult)
             po[sl] = bank(sl * MT, [P, NBT, SW], F32, "po%d" % sl)
+            nc.tensor.matmul(
+                out=po[sl][:], lhsT=ident_b[:], rhs=h_sb[:, :, sl * SW:(sl + 1) * SW], start=True, stop=False,
+            )
             for bt in range(NBT):
-                nc.tensor.matmul(
-                    out=po[sl][:, bt, :], lhsT=ident_b[:], rhs=h_sb[:, bt, sl * SW:(sl + 1) * SW],
-                    start=True, stop=False,
-                )
                 for i in range(MT):
                     nc.tensor.matmul(
                         out=po[sl][:, bt, i * P:(i + 1) * P],
@@ -368,7 +365,7 @@ def tile_attentiongrucell_pa_kernel(
                         rhs=ident_f[:],
                         is_transpose=True,
                         start=False,
-                        stop=(i == MT - 1),
+                        stop=(bt == NBT - 1 and i == MT - 1),
                     )
 
         def tail_c(sl):

from contextlib import ExitStack

import concourse.mybir as mybir
from concourse.masks import make_identity

F32 = mybir.dt.float32
BF16 = mybir.dt.bfloat16
U32 = mybir.dt.uint32
U8 = mybir.dt.uint8
FP8X4 = mybir.dt.float8_e4m3fn_x4
ACT = mybir.ActivationFunctionType
ALU = mybir.AluOpType

P = 128
B = 256
E = 1024
H = 1024
A = 2048
KP = 512
NBT = B // P
NM = H // P

FLOPS = 2 * B * (E + H + A) * H * 3

RAW_BUFS = 8
GRP_BUFS = 4
Q_BUFS = 10
SPLIT = 496
SPLIT_D = 416
DET_COLS = 256
NLIVE = 6
TAIL_CHUNKS = 2
NS = 4
SW = H // NS
MT = NM // NS
TAIL_V = 256


def tile_attentiongrucell_pa_kernel(
    tc, in_word, last_hid_state, attended_state,
    W, Wz, Wr, U, Uz, Ur, C, Cz, Cr,
    bw, bwz, bwr, bu, buz, bur, bc, bcz, bcr, out,
):
    nc = tc.nc
    with ExitStack() as ctx:
        const = ctx.enter_context(tc.tile_pool(name="const", bufs=1))
        rawp = ctx.enter_context(tc.tile_pool(name="rawp", bufs=RAW_BUFS))
        grpp = ctx.enter_context(tc.tile_pool(name="grpp", bufs=GRP_BUFS))
        qp = ctx.enter_context(tc.tile_pool(name="qp", bufs=Q_BUFS))
        ps = ctx.enter_context(tc.psum_pool(name="ps", bufs=1))

        def bank(i, shape, dtype, name):
            return ps.tile(shape, dtype, tag="bank%d" % i, name=name)

        vcopy = nc.vector.tensor_copy
        scopy = nc.scalar.copy

        chunks = []
        for gate, (wx, wh, wa) in enumerate(((Wr, Ur, Cr), (W, U, C), (Wz, Uz, Cz))):
            part_x = [(wx, g, False, ("act", g)) for g in range(E // KP)]
            part_a = [(wa, g, False, ("act", 4 + g)) for g in range(A // KP)]
            if gate == 1:
                part_h = [(wh, g, True, ("rh", g)) for g in range(H // KP)]
                parts = part_x + part_a + part_h
            else:
                part_h = [(wh, g, False, ("act", 2 + g)) for g in range(H // KP)]
                parts = part_x + part_h + part_a
            for n, (w, g, by128, mov) in enumerate(parts):
                chunks.append((w, g, by128, mov, gate, n == 0, n == len(parts) - 1))
        NCH = len(chunks)
        NPLAIN = NCH - TAIL_CHUNKS

        def is_det(c):
            gate, n = divmod(c, 8)
            return 0 <= c < NCH and 2 <= n <= (7 if gate < 2 else 5)

        ident_f = const.tile([P, P], F32, name="ident_f")
        make_identity(nc, ident_f[:])
        ident_b = const.tile([P, P], BF16, name="ident_b")
        btile = const.tile([P, P], BF16, name="btile")
        nc.vector.memset(btile[:], 0.0)
        warm_in = const.tile([P, 1], F32, name="warm_in")
        warm_out = const.tile([P, 1], F32, name="warm_out")
        nc.vector.memset(warm_in[:], 0.0)
        nc.vector.tensor_copy(out=ident_b[:], in_=ident_f[:])
        biases = (bwr, bw, bwz, bur, bu, buz, bcr, bc, bcz)

        def load_bias(n):
            nc.scalar.dma_start(
                out=btile[n * NM:(n + 1) * NM, :],
                in_=biases[n].rearrange("(i p) -> i p", p=P),
            )

        x_sb = const.tile([P, NBT, E], BF16, name="x_sb")
        h_sb = const.tile([P, NBT, H], BF16, name="h_sb")
        a_sb = const.tile([P, NBT, A], BF16, name="a_sb", tag="a_o")
        raw = {}

        def load(c):
            if c >= NCH:
                return
            w, g, by128 = chunks[c][0], chunks[c][1], chunks[c][2]
            t = rawp.tile([P, 4, H], BF16, name="raw%d" % c, tag="raw")
            rows = w[g * KP:(g + 1) * KP, :]
            if by128:
                src = rows.rearrange("(j p) n -> p j n", p=P)
            else:
                src = rows.rearrange("(p j) n -> p j n", j=4)
            nc.sync.dma_start(out=t[:], in_=src)
            raw[c] = t

        nc.sync.dma_start(out=x_sb[:], in_=in_word.rearrange("(t p) k -> p t k", p=P))
        for n in range(4):
            load_bias(n)
        nc.scalar.activation(out=warm_out[:], in_=warm_in[:], func=ACT.Sigmoid)
        load(0)
        nc.sync.dma_start(out=h_sb[:], in_=last_hid_state.rearrange("(t p) k -> p t k", p=P))
        load(1)
        for n in range(4, 9):
            load_bias(n)
        nc.sync.dma_start(out=a_sb[:], in_=attended_state.rearrange("(t p) k -> p t k", p=P))
        for c in range(2, RAW_BUFS):
            load(c)

        actg = const.tile([P, 8 * 4 * B], BF16, name="actg", align_bytes=64)
        actc = const.tile([P, 8 * B], U32, name="actc", align_bytes=64)
        acts = const.tile([P, 8 * B], U8, name="acts", align_bytes=64)
        hT = const.tile([P, NM, B], BF16, name="hT")
        bT = const.tile([P, 9 * NM], F32, name="bT")
        bsum = const.tile([P, 3 * NM], F32, name="bsum")
        r_sb = const.tile([P, NM, B], F32, name="r_sb", tag="r_z")
        c_sb = const.tile([P, NM, B], F32, name="c_sb")
        rhg = const.tile([P, 2 * 4 * B], BF16, name="rhg", align_bytes=64)
        rhc = const.tile([P, 2 * B], U32, name="rhc", align_bytes=64)
        rhs = const.tile([P, 2 * B], U8, name="rhs", align_bytes=64)
        grp = {}
        cod = {}
        scl = {}
        acc = {}
        det = {}

        def word_transposes(src_sb, g, bk, name):
            tw = bank(bk, [P, NBT, 2, P], F32, name)
            words = src_sb[:].bitcast(F32).rearrange("p t (g q u) -> p t g u q", q=P, u=2)
            for bt in range(NBT):
                for u in range(2):
                    nc.tensor.transpose(tw[:, bt, u, :], words[:, bt, g, u, :], ident_f[:])
            return tw

        def word_copy(copy, tw, pas):
            dst = actg[:, pas * 4 * B:(pas + 1) * 4 * B].bitcast(F32)
            copy(
                out=dst.rearrange("p (t b u) -> p t b u", t=NBT, u=2),
                in_=tw[:].rearrange("p t u b -> p t b u"),
            )

        def quant_act(p0, n):
            nc.vector.quantize_mx(
                out=actc[:, p0 * B:(p0 + n) * B].bitcast(FP8X4),
                scales=acts[:, p0 * B:(p0 + n) * B],
                in_=actg[:, p0 * 4 * B:(p0 + n) * 4 * B],
            )

        def h_transposes(half, bk):
            hps = bank(bk, [P, 4, B], BF16, "hps%d" % half)
            for i in range(4):
                for bt in range(NBT):
                    k0 = (half * 4 + i) * P
                    nc.tensor.transpose(
                        hps[:, i, bt * P:(bt + 1) * P], h_sb[:, bt, k0:k0 + P], ident_b[:]
                    )
            return hps

        def regroup_cols(copy, dst, src):
            copy(
                out=dst.rearrange("p (c i j) -> p c j i", i=8, j=4),
                in_=src.rearrange("p j (c i) -> p c j i", i=8),
            )

        def regroup(c):
            t = grpp.tile([P, 4 * H], BF16, name="grp%d" % c, tag="grp", align_bytes=64)
            grp[c] = t
            cut = SPLIT_D if is_det(c) else SPLIT
            top = H - DET_COLS if is_det(c) else H
            regroup_cols(vcopy, t[:, 0:4 * cut], raw[c][:, :, 0:cut])
            regroup_cols(scopy, t[:, 4 * cut:4 * top], raw[c][:, :, cut:top])
            if is_det(c):
                scopy(out=t[:, 4 * top:4 * H], in_=det[c][:].rearrange("p n j -> p (n j)"))
            load(c + RAW_BUFS)

        def detour(c):
            if not is_det(c):
                return
            det[c] = bank(NLIVE + c % 2, [P, DET_COLS, 4], BF16, "det%d" % c)
            for a in range(2):
                nc.tensor.matmul(
                    out=det[c][:, :, 2 * a:2 * a + 2].rearrange("p n j -> p j n"),
                    lhsT=ident_b[:],
                    rhs=raw[c][:, 2 * a:2 * a + 2, H - DET_COLS:H],
                    start=True,
                    stop=True,
                )

        def new_codes(c):
            cod[c] = qp.tile([P, H], U32, name="cod%d" % c, tag="cod", align_bytes=64)
            scl[c] = qp.tile([P, H], U8, name="scl%d" % c, tag="scl", align_bytes=64)

        def quant(c):
            new_codes(c)
            nc.vector.quantize_mx(out=cod[c][:].bitcast(FP8X4), scales=scl[c][:], in_=grp[c][:])

        def one_pass(c, m, codes, scales, col):
            mov, gate, first, last = chunks[c][3], chunks[c][4], chunks[c][5], chunks[c][6]
            kind, idx = mov
            mc, ms = (actc, acts) if kind == "act" else (rhc, rhs)
            if first:
                acc[m] = bank(m, [P, B], F32, "acc%d_%d" % (gate, m))
            nc.tensor.matmul_mx(
                out=acc[m][:],
                lhsT=codes[:, col:col + P].bitcast(FP8X4),
                lhsT_scale=scales[:, col:col + P],
                rhs=mc[:, idx * B:(idx + 1) * B].bitcast(FP8X4),
                rhs_scale=ms[:, idx * B:(idx + 1) * B],
                start=first,
                stop=last,
            )

        def passes(c):
            for m in range(NLIVE):
                one_pass(c, m, cod[c], scl[c], m * P)
            if chunks[c][6]:
                catch_up(c)

        def catch_up(c):
            for m in range(NLIVE, NM):
                for cc in range(c - c % 8, c + 1):
                    one_pass(cc, m, cod[cc], scl[cc], m * P)

        def gate_act(gate, m, dst, func):
            nc.scalar.activation(
                out=dst[:, m, :], in_=acc[m][:], func=func,
                bias=bsum[:, gate * NM + m:gate * NM + m + 1],
            )

        def rh_mul(g):
            nc.vector.tensor_tensor(
                out=rhg[:, g * 4 * B:(g + 1) * 4 * B].rearrange("p (c i t) -> p c t i", i=4, t=4),
                in0=r_sb[:, 4 * g:4 * g + 4, :].rearrange("p t (c i) -> p c t i", i=4),
                in1=hT[:, 4 * g:4 * g + 4, :].rearrange("p t (c i) -> p c t i", i=4),
                op=ALU.mult,
            )

        def c_minus_h(g):
            nc.vector.tensor_tensor(
                out=c_sb[:, 4 * g:4 * g + 4, :], in0=c_sb[:, 4 * g:4 * g + 4, :],
                in1=hT[:, 4 * g:4 * g + 4, :], op=ALU.subtract,
            )

        tx0 = word_transposes(x_sb, 0, 0, "tx0")
        tx1 = word_transposes(x_sb, 1, 1, "tx1")
        word_copy(vcopy, tx0, 0)
        word_copy(scopy, tx1, 1)
        th0 = word_transposes(h_sb, 0, 2, "th0")
        th1 = word_transposes(h_sb, 1, 3, "th1")
        hps0 = h_transposes(0, 4)
        hps1 = h_transposes(1, 5)
        ta0 = word_transposes(a_sb, 0, 0, "ta0")
        ta1 = word_transposes(a_sb, 1, 1, "ta1")
        quant_act(0, 2)
        regroup(0)
        word_copy(scopy, th0, 2)
        word_copy(vcopy, th1, 3)
        ta2 = word_transposes(a_sb, 2, 2, "ta2")
        ta3 = word_transposes(a_sb, 3, 3, "ta3")
        regroup(1)
        quant(0)
        scopy(out=hT[:, 0:4, :], in_=hps0[:])
        scopy(out=hT[:, 4:8, :], in_=hps1[:])
        bps = bank(4, [P, P], BF16, "bps")
        nc.tensor.transpose(bps[:], btile[:], ident_b[:])
        detour(2)
        quant_act(2, 2)
        regroup(2)
        quant(1)
        detour(3)
        word_copy(scopy, ta0, 4)
        word_copy(vcopy, ta1, 5)
        word_copy(scopy, ta2, 6)
        word_copy(vcopy, ta3, 7)
        regroup(3)
        quant(2)
        nc.vector.tensor_copy(out=bT[:], in_=bps[:, 0:9 * NM])
        nc.vector.tensor_tensor(out=bsum[:], in0=bT[:, 0:24], in1=bT[:, 24:48], op=ALU.add)
        nc.vector.tensor_tensor(out=bsum[:], in0=bsum[:], in1=bT[:, 48:72], op=ALU.add)
        quant_act(4, 4)
        detour(4)
        passes(0)
        passes(1)
        passes(2)

        for s in range(3, NPLAIN):
            if s + 1 < NPLAIN:
                regroup(s + 1)
            if s == 8:
                for m in range(NM):
                    gate_act(0, m, r_sb, ACT.Sigmoid)
            if s == 16:
                for m in range(NM):
                    gate_act(1, m, c_sb, ACT.Tanh)
            detour(s + 2)
            quant(s)
            passes(s)
            if s in (9, 10):
                rh_mul(s - 9)
            if s == 11:
                nc.vector.quantize_mx(out=rhc[:].bitcast(FP8X4), scales=rhs[:], in_=rhg[:])
            if s in (17, 18):
                c_minus_h(s - 17)

        out_v = out.rearrange("(t p) n -> p t n", p=P)
        po = {}
        z_sb = const.tile([P, NM, B], F32, name="z_sb", tag="r_z")
        o_sb = const.tile([P, NBT, H], F32, name="o_sb", tag="a_o")

        def tail_a(sl):
            if sl % 2 == 0:
                new_codes(NPLAIN + sl // 2)
            codes, scales = cod[NPLAIN + sl // 2], scl[NPLAIN + sl // 2]
            g0 = sl * TAIL_CHUNKS * 4 * SW
            for k in reversed(range(TAIL_CHUNKS)):
                src = raw[NPLAIN + k]
                dst = actg[:, g0 + k * 4 * SW:g0 + (k + 1) * 4 * SW]
                nv = TAIL_V if k == TAIL_CHUNKS - 1 else 0
                cut = SW - nv
                if cut > 0:
                    regroup_cols(scopy, dst[:, 0:4 * cut], src[:, :, sl * SW:sl * SW + cut])
                if nv > 0:
                    regroup_cols(vcopy, dst[:, 4 * cut:4 * SW], src[:, :, sl * SW + cut:(sl + 1) * SW])
            q0 = (sl % 2) * TAIL_CHUNKS * SW
            nc.vector.quantize_mx(
                out=codes[:, q0:q0 + TAIL_CHUNKS * SW].bitcast(FP8X4),
                scales=scales[:, q0:q0 + TAIL_CHUNKS * SW],
                in_=actg[:, g0:g0 + TAIL_CHUNKS * 4 * SW],
            )
            if sl == 1:
                catch_up(NPLAIN - 1)
            for i in range(MT):
                for k in range(TAIL_CHUNKS):
                    one_pass(NPLAIN + k, sl * MT + i, codes, scales, q0 + k * SW + i * P)

        def tail_b(sl):
            ms = slice(sl * MT, (sl + 1) * MT)
            for i in range(MT):
                gate_act(2, sl * MT + i, z_sb, ACT.Sigmoid)
            nc.vector.tensor_tensor(out=z_sb[:, ms, :], in0=z_sb[:, ms, :], in1=c_sb[:, ms, :], op=ALU.mult)
            po[sl] = bank(sl * MT, [P, NBT, SW], F32, "po%d" % sl)
            nc.tensor.matmul(
                out=po[sl][:], lhsT=ident_b[:], rhs=h_sb[:, :, sl * SW:(sl + 1) * SW], start=True, stop=False,
            )
            for bt in range(NBT):
                for i in range(MT):
                    nc.tensor.matmul(
                        out=po[sl][:, bt, i * P:(i + 1) * P],
                        lhsT=z_sb[:, sl * MT + i, bt * P:(bt + 1) * P],
                        rhs=ident_f[:],
                        is_transpose=True,
                        start=False,
                        stop=(bt == NBT - 1 and i == MT - 1),
                    )

        def tail_c(sl):
            cols = slice(sl * SW, (sl + 1) * SW)
            scopy(out=o_sb[:, :, cols], in_=po[sl][:])
            nc.sync.dma_start(out=out_v[:, :, cols], in_=o_sb[:, :, cols])

        for i in range(NS + 4):
            if i < NS:
                tail_a(i)
            if 0 <= i - 2 < NS:
                tail_b(i - 2)
            if 0 <= i - 4 < NS:
                tail_c(i - 4)
